import numpy as np
import ml_dtypes


def mxq(x, axis, fmt="e4m3"):
    dtype, down = {"e4m3": (ml_dtypes.float8_e4m3fn, 7), "e5m2": (ml_dtypes.float8_e5m2, 14)}[fmt]
    v = np.moveaxis(np.asarray(x, np.float32).astype(ml_dtypes.bfloat16).astype(np.float64), axis, -1)
    blocks = v.reshape(v.shape[:-1] + (-1, 32))
    amax = np.abs(blocks).max(-1, keepdims=True)
    byte = np.maximum(np.where(amax > 0, np.frexp(amax)[1] - 1 + 127, 0) - down, 1)
    scale = np.exp2(byte - 127.0)
    codes = (blocks / scale).astype(np.float32).astype(dtype).astype(np.float64)
    return np.moveaxis((codes * scale).reshape(v.shape), -1, axis)


WIDE = False


def mx_kscale(k):
    if not WIDE:
        return np.ones(k)
    levels = np.array([10, -10, 5, -5, 0])
    a = np.random.permutation(np.resize(levels, k // 512 * 4)).reshape(k // 512, 4)
    idx = np.arange(k)
    return np.exp2(a[idx // 512, idx % 128 // 32])


BF16 = ml_dtypes.bfloat16


def bf(x):
    return np.asarray(x, np.float32).astype(BF16)


def f64(x):
    return np.asarray(x).astype(np.float64)


E2M1 = np.array([0.0, 0.5, 1.0, 1.5, 2.0, 3.0, 4.0, 6.0, -0.0, -0.5, -1.0, -1.5, -2.0, -3.0, -4.0, -6.0])


def pack_weight(w, fmt):
    k, n = w.shape
    w = f64(bf(w)).reshape(k // 32, 32, n)
    amax = np.abs(w).max(1)
    if fmt == "e4m3":
        byte = np.frexp(amax)[1] - 1 + 127 - 7
    else:
        mant, ex = np.frexp(amax / 6.0)
        byte = np.where(mant > 0.5, ex, ex - 1) + 127
    byte = np.clip(np.where(amax > 0, byte, 1), 1, 254)
    scaled = (w * np.exp2(127.0 - byte)[:, None, :]).reshape(k, n).astype(np.float32)
    by_word = np.ascontiguousarray(scaled.reshape(k // 512, 128, 4, n).transpose(0, 1, 3, 2))
    if fmt == "e4m3":
        words = by_word.astype(ml_dtypes.float8_e4m3fn).view(np.uint8)
    else:
        c = by_word.astype(ml_dtypes.float4_e2m1fn).view(np.uint8) & 0xF
        words = c[..., 0::2] | (c[..., 1::2] << 4)
    return np.ascontiguousarray(words), np.ascontiguousarray(byte.astype(np.uint8).reshape(k // 512, 16, n))


def unpack_weight(words, scales, fmt):
    g, p, n, _ = words.shape
    if fmt == "e4m3":
        vals = np.ascontiguousarray(words).view(ml_dtypes.float8_e4m3fn).astype(np.float64)
    else:
        nib = np.empty((g, p, n, 4), np.uint8)
        nib[..., 0::2] = words & 0xF
        nib[..., 1::2] = words >> 4
        vals = E2M1[nib]
    vals = vals * np.repeat(np.exp2(scales.astype(np.float64) - 127.0), 8, axis=1)[..., None]
    return vals.transpose(0, 1, 3, 2).reshape(g * 512, n)


B, D, O1, O2, O3 = 4096, 768, 1024, 512, 128
EPS = 1e-5
FMT = "e4m3"


def mish(v):
    return v * np.tanh(np.log(1.0 + np.exp(v)))


def sigmoid(v):
    return 1.0 / (1.0 + np.exp(-v))


def ln(u, g, b):
    mu = u.mean(-1, keepdims=True)
    var = np.square(u - mu).mean(-1, keepdims=True)
    return (u - mu) * (1.0 / np.sqrt(var + EPS)) * g + b


def setup_inputs():
    s = mx_kscale(O2)
    h_dec1 = bf(mish(np.random.standard_normal((B, O2))) * s)
    d2 = np.random.standard_normal((O1, O2)) * 1.5 / np.sqrt(O2) / s
    D2_words, D2_scales = pack_weight(np.ascontiguousarray(d2.T), FMT)
    g4 = bf(1.0 + 0.1 * np.random.standard_normal(O1))
    b4 = bf(0.1 * np.random.standard_normal(O1))
    d3 = np.random.standard_normal((D, O1)) * 1.5 / np.sqrt(O1)
    D3_words, D3_scales = pack_weight(np.ascontiguousarray(d3.T), FMT)
    bo = bf(0.3 * np.random.standard_normal(D))
    return {"h_dec1": h_dec1,
            "D2_words": D2_words,
            "D2_scales": D2_scales,
            "g4": g4,
            "b4": b4,
            "D3_words": D3_words,
            "D3_scales": D3_scales,
            "bo": bo}


def reference(h_dec1, D2_words, D2_scales, g4, b4, D3_words, D3_scales, bo):
    u = mxq(f64(h_dec1), 1, "e4m3") @ unpack_weight(D2_words, D2_scales, FMT)
    h = mish(ln(u, f64(g4), f64(b4)))
    return sigmoid((mxq(h, 1, "e4m3") @ unpack_weight(D3_words, D3_scales, FMT)) + f64(bo))

@@ -1,0 +1,340 @@
+from contextlib import ExitStack
+
+import concourse.mybir as mybir
+from concourse.masks import make_identity
+
+F32 = mybir.dt.float32
+BF16 = mybir.dt.bfloat16
+U8 = mybir.dt.uint8
+U32 = mybir.dt.uint32
+I32 = mybir.dt.int32
+FP8X4 = mybir.dt.float8_e4m3fn_x4
+ACT = mybir.ActivationFunctionType
+ALU = mybir.AluOpType
+
+P = 128
+PACK = 4
+K_PASS = P * PACK
+BANK = 512
+
+ROWS = 4096
+K1 = 512
+N1 = 1024
+N2 = 768
+PASSES2 = N1 // K_PASS
+EPS = 1e-5
+GROUP = 4
+GROUPS = ROWS // (GROUP * P)
+TILES = GROUPS * GROUP
+AHEAD = 2
+LOG_FLOOR = 2.0**-60
+
+FLOPS = 2 * ROWS * K1 * N1 + 2 * ROWS * N1 * N2
+
+
+def tile_autoencoder_pb_t_kernel(
+    tc, h_dec1, D2_words, D2_scales, g4, b4, D3_words, D3_scales, bo, out
+):
+    nc = tc.nc
+    x_rows = h_dec1.rearrange("(c r a) k -> c r a k", r=P, a=GROUP)
+    out_rows = out.rearrange("(c r a) n -> c r a n", r=P, a=GROUP)
+
+    with ExitStack() as stack:
+        const = stack.enter_context(tc.tile_pool(name="const", bufs=1))
+        x_pool = stack.enter_context(tc.tile_pool(name="x", bufs=GROUPS))
+        x_mx_pool = stack.enter_context(tc.tile_pool(name="x_mx", bufs=3))
+        stat_pool = stack.enter_context(tc.tile_pool(name="stat", bufs=2 * GROUP))
+        centred_pool = stack.enter_context(tc.tile_pool(name="centred", bufs=GROUP))
+        chain_pool = stack.enter_context(tc.tile_pool(name="chain", bufs=2))
+        h_pool = stack.enter_context(tc.tile_pool(name="h", bufs=GROUP))
+        h_mx_pool = stack.enter_context(tc.tile_pool(name="h_mx", bufs=2 * GROUP))
+        out_pool = stack.enter_context(tc.tile_pool(name="o", bufs=2))
+        u_psum = stack.enter_context(tc.psum_pool(name="u_psum", bufs=2 * AHEAD))
+        turn_psum = stack.enter_context(tc.psum_pool(name="turn_psum", bufs=2))
+        y_psum = stack.enter_context(tc.psum_pool(name="y_psum", bufs=1))
+        stack.enter_context(tc.manual_schedule())
+
+        identity = const.tile([P, P], F32)
+        make_identity(nc, identity[:])
+        log_floor = const.tile([P, 1], F32)
+        nc.vector.memset(log_floor[:], LOG_FLOOR)
+        minus_half = const.tile([P, 1], F32)
+        nc.vector.memset(minus_half[:], -0.5)
+        table_scratch = const.tile([P, 1], F32)
+
+        w2_words = const.tile([P, N1], U32, align_bytes=64)
+        w2_scales = const.tile([P, N1], U8, align_bytes=64)
+        w3_words = const.tile([P, PASSES2, N2], U32, align_bytes=64)
+        w3_scales = const.tile([P, PASSES2, N2], U8, align_bytes=64)
+        nc.vector.memset(w2_scales[:].bitcast(I32), 0)
+        nc.vector.memset(w3_scales[:].bitcast(I32), 0)
+
+        x_tiles = {}
+
+        def load_x(c):
+            x_sb = x_pool.tile([P, GROUP, K1], BF16)
+            nc.sync.dma_start(out=x_sb[:], in_=x_rows[c])
+            x_tiles[c] = x_sb
+
+        def load_scales(plane, rows):
+            for quadrant in range(4):
+                nc.sync.dma_start(
+                    out=plane[32 * quadrant : 32 * quadrant + 4, :].bitcast(I32),
+                    in_=rows[4 * quadrant : 4 * quadrant + 4, :].bitcast(I32),
+                )
+
+        def load_words(words, packed):
+            nc.sync.dma_start(
+                out=words.bitcast(I32),
+                in_=packed.rearrange("p n t -> p (n t)").bitcast(I32),
+            )
+
+        load_x(0)
+        load_scales(w2_scales, D2_scales[0])
+        load_words(w2_words[:], D2_words[0])
+        load_x(1)
+        load_x(2)
+        for g in range(PASSES2):
+            load_scales(w3_scales[:, g, :], D3_scales[g])
+        for g in range(PASSES2):
+            load_words(w3_words[:, g, :], D3_words[g])
+        for c in range(3, GROUPS):
+            load_x(c)
+
+        gain_bc = const.tile([P, N1], BF16)
+        nc.scalar.dma_start(out=gain_bc[:], in_=g4.partition_broadcast(P))
+        bias_bc = const.tile([P, N1], BF16)
+        nc.scalar.dma_start(out=bias_bc[:], in_=b4.partition_broadcast(P))
+        out_bias_bc = const.tile([P, N2], BF16)
+        nc.scalar.dma_start(out=out_bias_bc[:], in_=bo.partition_broadcast(P))
+
+        def valid(c):
+            return 0 <= c < GROUPS
+
+        x_turned = {}
+        x_codes = {}
+        x_scales = {}
+
+        def turn_x(c):
+            words = x_tiles[c][:].bitcast(F32)
+            banks = []
+            for pair in range(GROUP // 2):
+                x_bank = turn_psum.tile([P, 2, 2 * P], F32, tag="turn")
+                for i in range(2):
+                    for e2 in range(2):
+                        nc.tensor.transpose(
+                            x_bank[:, e2, i * P : (i + 1) * P],
+                            words[:, 2 * pair + i, e2 : K1 // 2 : 2],
+                            identity[:],
+                        )
+                banks.append(x_bank)
+            x_turned[c] = banks
+
+        def quantise_x(c):
+            grouped = x_mx_pool.tile([P, GROUP * P * PACK], BF16, align_bytes=64)
+            grouped_words = grouped[:].bitcast(F32).rearrange("p (w e2) -> p w e2", e2=2)
+            for pair in range(GROUP // 2):
+                nc.vector.tensor_copy(
+                    out=grouped_words[:, 2 * pair * P : 2 * (pair + 1) * P, :],
+                    in_=x_turned[c][pair][:].rearrange("p e2 w -> p w e2"),
+                )
+            codes = x_mx_pool.tile([P, GROUP * P], U32, align_bytes=64)
+            scales = x_mx_pool.tile([P, GROUP * P], U8, align_bytes=64)
+            nc.vector.quantize_mx(out=codes[:].bitcast(FP8X4), scales=scales[:], in_=grouped[:])
+            x_codes[c] = codes
+            x_scales[c] = scales
+
+        u_banks = {}
+        mean_vars = {}
+        rstds = {}
+        centreds = {}
+        v_tiles = {}
+
+        def first_product(j):
+            c, a = divmod(j, GROUP)
+            rows = slice(a * P, (a + 1) * P)
+            banks = []
+            for half in range(N1 // BANK):
+                cols = slice(half * BANK, (half + 1) * BANK)
+                u_bank = u_psum.tile([P, BANK], F32, tag="u")
+                nc.tensor.matmul_mx(
+                    out=u_bank[:],
+                    lhsT=x_codes[c][:, rows].bitcast(FP8X4),
+                    lhsT_scale=x_scales[c][:, rows],
+                    rhs=w2_words[:, cols].bitcast(FP8X4),
+                    rhs_scale=w2_scales[:, cols],
+                    start=True,
+                    stop=True,
+                )
+                banks.append(u_bank)
+            u_banks[j] = banks
+
+        def statistics(j):
+            stats = stat_pool.tile([P, N1 // BANK, 6], F32)
+            for half in range(N1 // BANK):
+                nc.vector.bn_stats(out=stats[:, half, :], in_=u_banks[j][half][:])
+            mean_var = stat_pool.tile([P, 2], F32)
+            nc.vector.bn_aggr(out=mean_var[:], in_=stats[:].rearrange("p h s -> p (h s)"))
+            var_eps = stat_pool.tile([P, 1], F32)
+            nc.gpsimd.tensor_scalar(
+                out=var_eps[:], in0=mean_var[:, 1:2], scalar1=1.0, scalar2=EPS,
+                op0=ALU.mult, op1=ALU.add,
+            )
+            rstd = stat_pool.tile([P, 1], F32)
+            nc.gpsimd.tensor_tensor(out=rstd[:], in0=var_eps[:], in1=minus_half[:], op=ALU.pow)
+            mean_vars[j] = mean_var
+            rstds[j] = rstd
+
+        def centre_and_gain(j):
+            centred = centred_pool.tile([P, N1], F32)
+            for half in range(N1 // BANK):
+                cols = slice(half * BANK, (half + 1) * BANK)
+                nc.vector.scalar_tensor_tensor(
+                    out=centred[:, cols], in0=u_banks[j][half][:], scalar=mean_vars[j][:, 0:1],
+                    in1=gain_bc[:, cols], op0=ALU.subtract, op1=ALU.mult,
+                )
+            centreds[j] = centred
+
+        def scale_and_bias(j):
+            c, a = divmod(j, GROUP)
+            if a == 0:
+                v_group = chain_pool.tile([P, GROUP, N1], F32)
+                v_tiles[c] = v_group
+            nc.vector.scalar_tensor_tensor(
+                out=v_tiles[c][:, a, :], in0=centreds[j][:], scalar=rstds[j][:, 0:1],
+                in1=bias_bc[:], op0=ALU.mult, op1=ALU.add,
+            )
+
+        t_tiles = {}
+        h_tiles = {}
+
+        def sigmoid_of_minus_v(c):
+            t_group = chain_pool.tile([P, GROUP, N1], F32)
+            t_tiles[c] = t_group
+            for first in range(0, GROUP, 2):
+                part = slice(first, first + 2)
+                nc.scalar.activation(
+                    out=t_group[:, part, :], in_=v_tiles[c][:, part, :], func=ACT.Sigmoid, scale=-1.0
+                )
+
+        def logarithm(c):
+            for first in range(0, GROUP, 2):
+                part = t_tiles[c][:, first : first + 2, :]
+                nc.scalar.activation(out=part, in_=part, func=ACT.Ln, bias=log_floor[:, 0:1])
+            nc.scalar.activation(out=table_scratch[:], in_=log_floor[:], func=ACT.Sigmoid)
+
+        def tanh_and_multiply(c, a):
+            part = t_tiles[c][:, a, :]
+            nc.scalar.activation(out=part, in_=part, func=ACT.Tanh, scale=-1.0)
+            h_bf = h_pool.tile([P, N1], BF16)
+            nc.gpsimd.tensor_tensor(out=h_bf[:], in0=v_tiles[c][:, a, :], in1=part, op=ALU.mult)
+            h_tiles[c * GROUP + a] = h_bf
+
+        h_groupeds = {}
+        h_codes = {}
+        h_scales = {}
+
+        def turn_h(j):
+            words = h_tiles[j][:].bitcast(F32)
+            h_bank = turn_psum.tile([P, PASSES2, 2, P], F32, tag="turn")
+            for g in range(PASSES2):
+                for e2 in range(2):
+                    nc.tensor.transpose(
+                        h_bank[:, g, e2, :],
+                        words[:, g * K_PASS // 2 + e2 : (g + 1) * K_PASS // 2 : 2],
+                        identity[:],
+                    )
+            grouped = h_mx_pool.tile([P, PASSES2 * P * PACK], BF16, align_bytes=64)
+            nc.scalar.copy(
+                out=grouped[:].bitcast(F32).rearrange("p (g r e2) -> p g r e2", g=PASSES2, e2=2),
+                in_=h_bank[:].rearrange("p g e2 r -> p g r e2"),
+            )
+            h_groupeds[j] = grouped
+
+        def quantise_h(j):
+            codes = h_mx_pool.tile([P, PASSES2 * P], U32, align_bytes=64)
+            scales = h_mx_pool.tile([P, PASSES2 * P], U8, align_bytes=64)
+            nc.vector.quantize_mx(
+                out=codes[:].bitcast(FP8X4), scales=scales[:], in_=h_groupeds[j][:]
+            )
+            h_codes[j] = codes
+            h_scales[j] = scales
+
+        y_banks = {}
+        o_tiles = {}
+        y_columns = (slice(0, BANK), slice(BANK, N2))
+
+        def second_product(j):
+            y_wide = y_psum.tile([P, BANK], F32)
+            y_narrow = y_psum.tile([P, N2 - BANK], F32)
+            y_banks[j] = (y_wide, y_narrow)
+            for g in range(PASSES2):
+                rows = slice(g * P, (g + 1) * P)
+                for y_bank, cols in zip(y_banks[j], y_columns):
+                    nc.tensor.matmul_mx(
+                        out=y_bank[:],
+                        lhsT=h_codes[j][:, rows].bitcast(FP8X4),
+                        lhsT_scale=h_scales[j][:, rows],
+                        rhs=w3_words[:, g, cols].bitcast(FP8X4),
+                        rhs_scale=w3_scales[:, g, cols],
+                        start=(g == 0),
+                        stop=(g == PASSES2 - 1),
+                    )
+
+        def add_out_bias(j):
+            c, a = divmod(j, GROUP)
+            if a == 0:
+                o_group = out_pool.tile([P, GROUP, N2], F32)
+                o_tiles[c] = o_group
+            for y_bank, cols in zip(y_banks[j], y_columns):
+                nc.vector.tensor_tensor(
+                    out=o_tiles[c][:, a, cols], in0=y_bank[:], in1=out_bias_bc[:, cols], op=ALU.add
+                )
+
+        def sigmoid_and_store(c):
+            for a in range(GROUP):
+                part = o_tiles[c][:, a, :]
+                nc.scalar.activation(out=part, in_=part, func=ACT.Sigmoid)
+            nc.sync.dma_start(out=out_rows[c], in_=o_tiles[c][:])
+
+        for c in range(2):
+            turn_x(c)
+            quantise_x(c)
+        for j in range(AHEAD):
+            first_product(j)
+
+        for c in range(-1, GROUPS + 1):
+            front, chain, back = c + 1, c, c - 1
+            if valid(back):
+                for a in range(GROUP):
+                    turn_h(back * GROUP + a)
+            if valid(chain):
+                sigmoid_of_minus_v(chain)
+            if valid(front):
+                for a in range(GROUP):
+                    j = front * GROUP + a
+                    statistics(j)
+                    centre_and_gain(j)
+                    if j + AHEAD < TILES:
+                        first_product(j + AHEAD)
+            if valid(c + 3):
+                turn_x(c + 3)
+            if valid(back):
+                for a in range(GROUP):
+                    quantise_h(back * GROUP + a)
+            if valid(chain):
+                logarithm(chain)
+            for a in range(GROUP):
+                if valid(back):
+                    second_product(back * GROUP + a)
+                if valid(front):
+                    scale_and_bias(front * GROUP + a)
+                if valid(back):
+                    add_out_bias(back * GROUP + a)
+            if valid(c + 3):
+                quantise_x(c + 3)
+            if valid(chain):
+                for a in range(GROUP):
+                    tanh_and_multiply(chain, a)
+            if valid(back):
+                sigmoid_and_store(back)

@@ -112,6 +112,7 @@ def tile_autoencoder_pb_t_kernel(
             return 0 <= c < GROUPS
 
         x_turned = {}
+        x_groupeds = {}
         x_codes = {}
         x_scales = {}
 
@@ -130,17 +131,22 @@ def tile_autoencoder_pb_t_kernel(
                 banks.append(x_bank)
             x_turned[c] = banks
 
-        def quantise_x(c):
+        def regroup_x(c):
             grouped = x_mx_pool.tile([P, GROUP * P * PACK], BF16, align_bytes=64)
             grouped_words = grouped[:].bitcast(F32).rearrange("p (w e2) -> p w e2", e2=2)
             for pair in range(GROUP // 2):
-                nc.vector.tensor_copy(
+                nc.scalar.copy(
                     out=grouped_words[:, 2 * pair * P : 2 * (pair + 1) * P, :],
                     in_=x_turned[c][pair][:].rearrange("p e2 w -> p w e2"),
                 )
+            x_groupeds[c] = grouped
+
+        def quantise_x(c):
             codes = x_mx_pool.tile([P, GROUP * P], U32, align_bytes=64)
             scales = x_mx_pool.tile([P, GROUP * P], U8, align_bytes=64)
-            nc.vector.quantize_mx(out=codes[:].bitcast(FP8X4), scales=scales[:], in_=grouped[:])
+            nc.vector.quantize_mx(
+                out=codes[:].bitcast(FP8X4), scales=scales[:], in_=x_groupeds[c][:]
+            )
             x_codes[c] = codes
             x_scales[c] = scales
 
@@ -230,6 +236,7 @@ def tile_autoencoder_pb_t_kernel(
             nc.gpsimd.tensor_tensor(out=h_bf[:], in0=v_tiles[c][:, a, :], in1=part, op=ALU.mult)
             h_tiles[c * GROUP + a] = h_bf
 
+        h_turned = {}
         h_groupeds = {}
         h_codes = {}
         h_scales = {}
@@ -244,10 +251,13 @@ def tile_autoencoder_pb_t_kernel(
                         words[:, g * K_PASS // 2 + e2 : (g + 1) * K_PASS // 2 : 2],
                         identity[:],
                     )
+            h_turned[j] = h_bank
+
+        def regroup_h(j):
             grouped = h_mx_pool.tile([P, PASSES2 * P * PACK], BF16, align_bytes=64)
-            nc.scalar.copy(
+            nc.vector.tensor_copy(
                 out=grouped[:].bitcast(F32).rearrange("p (g r e2) -> p g r e2", g=PASSES2, e2=2),
-                in_=h_bank[:].rearrange("p g e2 r -> p g r e2"),
+                in_=h_turned[j][:].rearrange("p g e2 r -> p g r e2"),
             )
             h_groupeds[j] = grouped
 
@@ -292,38 +302,47 @@ def tile_autoencoder_pb_t_kernel(
                 )
 
         def sigmoid_and_store(c):
-            for a in range(GROUP):
-                part = o_tiles[c][:, a, :]
+            for first in range(0, GROUP, 2):
+                part = o_tiles[c][:, first : first + 2, :]
                 nc.scalar.activation(out=part, in_=part, func=ACT.Sigmoid)
-            nc.sync.dma_start(out=out_rows[c], in_=o_tiles[c][:])
+                nc.sync.dma_start(out=out_rows[c][:, first : first + 2, :], in_=part)
 
-        for c in range(2):
-            turn_x(c)
-            quantise_x(c)
+        turn_x(0)
+        regroup_x(0)
+        quantise_x(0)
         for j in range(AHEAD):
             first_product(j)
+        turn_x(1)
+        regroup_x(1)
 
         for c in range(-1, GROUPS + 1):
             front, chain, back = c + 1, c, c - 1
-            if valid(back):
-                for a in range(GROUP):
-                    turn_h(back * GROUP + a)
             if valid(chain):
                 sigmoid_of_minus_v(chain)
-            if valid(front):
-                for a in range(GROUP):
-                    j = front * GROUP + a
-                    statistics(j)
-                    centre_and_gain(j)
-                    if j + AHEAD < TILES:
-                        first_product(j + AHEAD)
-            if valid(c + 3):
-                turn_x(c + 3)
+            if valid(c + 2):
+                quantise_x(c + 2)
+            for first in range(0, GROUP, 2):
+                pair = range(first, first + 2)
+                if valid(back):
+                    for a in pair:
+                        turn_h(back * GROUP + a)
+                if valid(front):
+                    for a in pair:
+                        j = front * GROUP + a
+                        statistics(j)
+                        centre_and_gain(j)
+                        if j + AHEAD < TILES:
+                            first_product(j + AHEAD)
+                if valid(back):
+                    for a in pair:
+                        regroup_h(back * GROUP + a)
             if valid(back):
                 for a in range(GROUP):
                     quantise_h(back * GROUP + a)
             if valid(chain):
                 logarithm(chain)
+            if valid(c + 3):
+                turn_x(c + 3)
             for a in range(GROUP):
                 if valid(back):
                     second_product(back * GROUP + a)
@@ -331,10 +350,10 @@ def tile_autoencoder_pb_t_kernel(
                     scale_and_bias(front * GROUP + a)
                 if valid(back):
                     add_out_bias(back * GROUP + a)
-            if valid(c + 3):
-                quantise_x(c + 3)
             if valid(chain):
                 for a in range(GROUP):
                     tanh_and_multiply(chain, a)
+            if valid(c + 3):
+                regroup_x(c + 3)
             if valid(back):
                 sigmoid_and_store(back)

@@ -233,7 +233,7 @@ def tile_autoencoder_pb_t_kernel(
             part = t_tiles[c][:, a, :]
             nc.scalar.activation(out=part, in_=part, func=ACT.Tanh, scale=-1.0)
             h_bf = h_pool.tile([P, N1], BF16)
-            nc.gpsimd.tensor_tensor(out=h_bf[:], in0=v_tiles[c][:, a, :], in1=part, op=ALU.mult)
+            nc.vector.tensor_tensor(out=h_bf[:], in0=v_tiles[c][:, a, :], in1=part, op=ALU.mult)
             h_tiles[c * GROUP + a] = h_bf
 
         h_turned = {}

@@ -22,34 +22,44 @@ K1 = 512
 N1 = 1024
 N2 = 768
 PASSES2 = N1 // K_PASS
+HALVES = N1 // BANK
 EPS = 1e-5
+TILES = ROWS // P
+PAIRS = TILES // 2
 GROUP = 4
-GROUPS = ROWS // (GROUP * P)
-TILES = GROUPS * GROUP
+GROUPS = TILES // GROUP
 AHEAD = 2
 LOG_FLOOR = 2.0**-60
 
 FLOPS = 2 * ROWS * K1 * N1 + 2 * ROWS * N1 * N2
 
 
+def tiles_of(c):
+    return [c * GROUP + a for a in range(GROUP)] if 0 <= c < GROUPS else []
+
+
+def pairs_of(c):
+    return [j // 2 for j in tiles_of(c)[::2]]
+
+
 def tile_autoencoder_pb_t_kernel(
     tc, h_dec1, D2_words, D2_scales, g4, b4, D3_words, D3_scales, bo, out
 ):
     nc = tc.nc
-    x_rows = h_dec1.rearrange("(c r a) k -> c r a k", r=P, a=GROUP)
-    out_rows = out.rearrange("(c r a) n -> c r a n", r=P, a=GROUP)
+    x_rows = h_dec1.rearrange("(p r i) k -> p r i k", r=P, i=2)
+    out_rows = out.rearrange("(p r i) n -> p r i n", r=P, i=2)
 
     with ExitStack() as stack:
         const = stack.enter_context(tc.tile_pool(name="const", bufs=1))
-        x_pool = stack.enter_context(tc.tile_pool(name="x", bufs=GROUPS))
-        x_mx_pool = stack.enter_context(tc.tile_pool(name="x_mx", bufs=3))
+        x_pool = stack.enter_context(tc.tile_pool(name="x", bufs=PAIRS))
+        x_mx_pool = stack.enter_context(tc.tile_pool(name="x_mx", bufs=3 * GROUP // 2))
         stat_pool = stack.enter_context(tc.tile_pool(name="stat", bufs=2 * GROUP))
         centred_pool = stack.enter_context(tc.tile_pool(name="centred", bufs=GROUP))
-        chain_pool = stack.enter_context(tc.tile_pool(name="chain", bufs=2))
+        chain_pool = stack.enter_context(tc.tile_pool(name="chain", bufs=GROUP))
         h_pool = stack.enter_context(tc.tile_pool(name="h", bufs=GROUP))
-        h_mx_pool = stack.enter_context(tc.tile_pool(name="h_mx", bufs=2 * GROUP))
-        out_pool = stack.enter_context(tc.tile_pool(name="o", bufs=2))
-        u_psum = stack.enter_context(tc.psum_pool(name="u_psum", bufs=2 * AHEAD))
+        h_mx_pool = stack.enter_context(tc.tile_pool(name="h_mx", bufs=GROUP))
+        out_pool = stack.enter_context(tc.tile_pool(name="o", bufs=GROUP))
+        u_psum = stack.enter_context(tc.psum_pool(name="u_psum", bufs=HALVES * AHEAD))
         turn_psum = stack.enter_context(tc.psum_pool(name="turn_psum", bufs=2))
         y_psum = stack.enter_context(tc.psum_pool(name="y_psum", bufs=1))
         stack.enter_context(tc.manual_schedule())
@@ -71,10 +81,10 @@ def tile_autoencoder_pb_t_kernel(
 
         x_tiles = {}
 
-        def load_x(c):
-            x_sb = x_pool.tile([P, GROUP, K1], BF16)
-            nc.sync.dma_start(out=x_sb[:], in_=x_rows[c])
-            x_tiles[c] = x_sb
+        def load_x(p):
+            x_sb = x_pool.tile([P, 2, K1], BF16)
+            nc.sync.dma_start(out=x_sb[:], in_=x_rows[p])
+            x_tiles[p] = x_sb
 
         def load_scales(plane, rows):
             for quadrant in range(4):
@@ -89,17 +99,19 @@ def tile_autoencoder_pb_t_kernel(
                 in_=packed.rearrange("p n t -> p (n t)").bitcast(I32),
             )
 
-        load_x(0)
+        for p in pairs_of(0):
+            load_x(p)
         load_scales(w2_scales, D2_scales[0])
         load_words(w2_words[:], D2_words[0])
-        load_x(1)
-        load_x(2)
+        for p in pairs_of(1) + pairs_of(2):
+            load_x(p)
         for g in range(PASSES2):
             load_scales(w3_scales[:, g, :], D3_scales[g])
         for g in range(PASSES2):
             load_words(w3_words[:, g, :], D3_words[g])
         for c in range(3, GROUPS):
-            load_x(c)
+            for p in pairs_of(c):
+                load_x(p)
 
         gain_bc = const.tile([P, N1], BF16)
         nc.scalar.dma_start(out=gain_bc[:], in_=g4.partition_broadcast(P))
@@ -108,65 +120,58 @@ def tile_autoencoder_pb_t_kernel(
         out_bias_bc = const.tile([P, N2], BF16)
         nc.scalar.dma_start(out=out_bias_bc[:], in_=bo.partition_broadcast(P))
 
-        def valid(c):
-            return 0 <= c < GROUPS
-
         x_turned = {}
         x_groupeds = {}
         x_codes = {}
         x_scales = {}
 
-        def turn_x(c):
-            words = x_tiles[c][:].bitcast(F32)
-            banks = []
-            for pair in range(GROUP // 2):
-                x_bank = turn_psum.tile([P, 2, 2 * P], F32, tag="turn")
-                for i in range(2):
-                    for e2 in range(2):
-                        nc.tensor.transpose(
-                            x_bank[:, e2, i * P : (i + 1) * P],
-                            words[:, 2 * pair + i, e2 : K1 // 2 : 2],
-                            identity[:],
-                        )
-                banks.append(x_bank)
-            x_turned[c] = banks
+        def turn_x(p):
+            words = x_tiles[p][:].bitcast(F32)
+            x_bank = turn_psum.tile([P, 2, 2 * P], F32, tag="turn")
+            for i in range(2):
+                for e2 in range(2):
+                    nc.tensor.transpose(
+                        x_bank[:, e2, i * P : (i + 1) * P], words[:, i, e2 : K1 // 2 : 2], identity[:]
+                    )
+            x_turned[p] = x_bank
 
-        def regroup_x(c):
-            grouped = x_mx_pool.tile([P, GROUP * P * PACK], BF16, align_bytes=64)
-            grouped_words = grouped[:].bitcast(F32).rearrange("p (w e2) -> p w e2", e2=2)
-            for pair in range(GROUP // 2):
-                nc.scalar.copy(
-                    out=grouped_words[:, 2 * pair * P : 2 * (pair + 1) * P, :],
-                    in_=x_turned[c][pair][:].rearrange("p e2 w -> p w e2"),
-                )
-            x_groupeds[c] = grouped
-
-        def quantise_x(c):
-            codes = x_mx_pool.tile([P, GROUP * P], U32, align_bytes=64)
-            scales = x_mx_pool.tile([P, GROUP * P], U8, align_bytes=64)
-            nc.vector.quantize_mx(
-                out=codes[:].bitcast(FP8X4), scales=scales[:], in_=x_groupeds[c][:]
+        def regroup_x(p):
+            grouped = x_mx_pool.tile([P, 2 * P * PACK], BF16, align_bytes=64)
+            nc.scalar.copy(
+                out=grouped[:].bitcast(F32).rearrange("q (w e2) -> q w e2", e2=2),
+                in_=x_turned[p][:].rearrange("q e2 w -> q w e2"),
             )
-            x_codes[c] = codes
-            x_scales[c] = scales
+            x_groupeds[p] = grouped
+
+        def quantise_x(p):
+            codes = x_mx_pool.tile([P, 2 * P], U32, align_bytes=64)
+            scales = x_mx_pool.tile([P, 2 * P], U8, align_bytes=64)
+            nc.vector.quantize_mx(
+                out=codes[:].bitcast(FP8X4), scales=scales[:], in_=x_groupeds[p][:]
+            )
+            x_codes[p] = codes
+            x_scales[p] = scales
 
         u_banks = {}
+        stats_of = {}
         mean_vars = {}
         rstds = {}
         centreds = {}
-        v_tiles = {}
+        v_pairs = {}
 
         def first_product(j):
-            c, a = divmod(j, GROUP)
-            rows = slice(a * P, (a + 1) * P)
+            if j >= TILES:
+                return
+            p, i = divmod(j, 2)
+            rows = slice(i * P, (i + 1) * P)
             banks = []
-            for half in range(N1 // BANK):
+            for half in range(HALVES):
                 cols = slice(half * BANK, (half + 1) * BANK)
                 u_bank = u_psum.tile([P, BANK], F32, tag="u")
                 nc.tensor.matmul_mx(
                     out=u_bank[:],
-                    lhsT=x_codes[c][:, rows].bitcast(FP8X4),
-                    lhsT_scale=x_scales[c][:, rows],
+                    lhsT=x_codes[p][:, rows].bitcast(FP8X4),
+                    lhsT_scale=x_scales[p][:, rows],
                     rhs=w2_words[:, cols].bitcast(FP8X4),
                     rhs_scale=w2_scales[:, cols],
                     start=True,
@@ -175,12 +180,19 @@ def tile_autoencoder_pb_t_kernel(
                 banks.append(u_bank)
             u_banks[j] = banks
 
-        def statistics(j):
-            stats = stat_pool.tile([P, N1 // BANK, 6], F32)
-            for half in range(N1 // BANK):
+        def bank_statistics(j):
+            if j >= TILES:
+                return
+            stats = stat_pool.tile([P, HALVES, 6], F32)
+            for half in range(HALVES):
                 nc.vector.bn_stats(out=stats[:, half, :], in_=u_banks[j][half][:])
+            stats_of[j] = stats
+
+        def mean_and_rstd(j):
+            if j >= TILES:
+                return
             mean_var = stat_pool.tile([P, 2], F32)
-            nc.vector.bn_aggr(out=mean_var[:], in_=stats[:].rearrange("p h s -> p (h s)"))
+            nc.vector.bn_aggr(out=mean_var[:], in_=stats_of[j][:].rearrange("r h s -> r (h s)"))
             var_eps = stat_pool.tile([P, 1], F32)
             nc.gpsimd.tensor_scalar(
                 out=var_eps[:], in0=mean_var[:, 1:2], scalar1=1.0, scalar2=EPS,
@@ -193,7 +205,7 @@ def tile_autoencoder_pb_t_kernel(
 
         def centre_and_gain(j):
             centred = centred_pool.tile([P, N1], F32)
-            for half in range(N1 // BANK):
+            for half in range(HALVES):
                 cols = slice(half * BANK, (half + 1) * BANK)
                 nc.vector.scalar_tensor_tensor(
                     out=centred[:, cols], in0=u_banks[j][half][:], scalar=mean_vars[j][:, 0:1],
@@ -202,41 +214,42 @@ def tile_autoencoder_pb_t_kernel(
             centreds[j] = centred
 
         def scale_and_bias(j):
-            c, a = divmod(j, GROUP)
-            if a == 0:
-                v_group = chain_pool.tile([P, GROUP, N1], F32)
-                v_tiles[c] = v_group
+            p, i = divmod(j, 2)
+            if i == 0:
+                v_pair = chain_pool.tile([P, 2, N1], F32)
+                v_pairs[p] = v_pair
             nc.vector.scalar_tensor_tensor(
-                out=v_tiles[c][:, a, :], in0=centreds[j][:], scalar=rstds[j][:, 0:1],
+                out=v_pairs[p][:, i, :], in0=centreds[j][:], scalar=rstds[j][:, 0:1],
                 in1=bias_bc[:], op0=ALU.mult, op1=ALU.add,
             )
 
-        t_tiles = {}
+        t_pairs = {}
         h_tiles = {}
 
-        def sigmoid_of_minus_v(c):
-            t_group = chain_pool.tile([P, GROUP, N1], F32)
-            t_tiles[c] = t_group
-            for first in range(0, GROUP, 2):
-                part = slice(first, first + 2)
-                nc.scalar.activation(
-                    out=t_group[:, part, :], in_=v_tiles[c][:, part, :], func=ACT.Sigmoid, scale=-1.0
-                )
+        def sigmoid_of_minus_v(p):
+            t_pair = chain_pool.tile([P, 2, N1], F32)
+            nc.scalar.activation(out=t_pair[:], in_=v_pairs[p][:], func=ACT.Sigmoid, scale=-1.0)
+            t_pairs[p] = t_pair
 
-        def logarithm(c):
-            for first in range(0, GROUP, 2):
-                part = t_tiles[c][:, first : first + 2, :]
-                nc.scalar.activation(out=part, in_=part, func=ACT.Ln, bias=log_floor[:, 0:1])
+        def logarithm(p):
+            nc.scalar.activation(
+                out=t_pairs[p][:], in_=t_pairs[p][:], func=ACT.Ln, bias=log_floor[:, 0:1]
+            )
+
+        def call_sigmoid_table():
             nc.scalar.activation(out=table_scratch[:], in_=log_floor[:], func=ACT.Sigmoid)
 
-        def tanh_and_multiply(c, a):
-            part = t_tiles[c][:, a, :]
-            nc.scalar.activation(out=part, in_=part, func=ACT.Tanh, scale=-1.0)
-            h_bf = h_pool.tile([P, N1], BF16)
-            nc.vector.tensor_tensor(out=h_bf[:], in0=v_tiles[c][:, a, :], in1=part, op=ALU.mult)
-            h_tiles[c * GROUP + a] = h_bf
+        def tanh_of_minus_log(p):
+            nc.scalar.activation(out=t_pairs[p][:], in_=t_pairs[p][:], func=ACT.Tanh, scale=-1.0)
 
-        h_turned = {}
+        def multiply(j):
+            p, i = divmod(j, 2)
+            h_bf = h_pool.tile([P, N1], BF16)
+            nc.vector.tensor_tensor(
+                out=h_bf[:], in0=v_pairs[p][:, i, :], in1=t_pairs[p][:, i, :], op=ALU.mult
+            )
+            h_tiles[j] = h_bf
+
         h_groupeds = {}
         h_codes = {}
         h_scales = {}
@@ -251,13 +264,10 @@ def tile_autoencoder_pb_t_kernel(
                         words[:, g * K_PASS // 2 + e2 : (g + 1) * K_PASS // 2 : 2],
                         identity[:],
                     )
-            h_turned[j] = h_bank
-
-        def regroup_h(j):
             grouped = h_mx_pool.tile([P, PASSES2 * P * PACK], BF16, align_bytes=64)
-            nc.vector.tensor_copy(
-                out=grouped[:].bitcast(F32).rearrange("p (g r e2) -> p g r e2", g=PASSES2, e2=2),
-                in_=h_turned[j][:].rearrange("p g e2 r -> p g r e2"),
+            nc.scalar.copy(
+                out=grouped[:].bitcast(F32).rearrange("q (g r e2) -> q g r e2", g=PASSES2, e2=2),
+                in_=h_bank[:].rearrange("q g e2 r -> q g r e2"),
             )
             h_groupeds[j] = grouped
 
@@ -271,7 +281,7 @@ def tile_autoencoder_pb_t_kernel(
             h_scales[j] = scales
 
         y_banks = {}
-        o_tiles = {}
+        o_pairs = {}
         y_columns = (slice(0, BANK), slice(BANK, N2))
 
         def second_product(j):
@@ -292,68 +302,64 @@ def tile_autoencoder_pb_t_kernel(
                     )
 
         def add_out_bias(j):
-            c, a = divmod(j, GROUP)
-            if a == 0:
-                o_group = out_pool.tile([P, GROUP, N2], F32)
-                o_tiles[c] = o_group
+            p, i = divmod(j, 2)
+            if i == 0:
+                o_pair = out_pool.tile([P, 2, N2], F32)
+                o_pairs[p] = o_pair
             for y_bank, cols in zip(y_banks[j], y_columns):
                 nc.vector.tensor_tensor(
-                    out=o_tiles[c][:, a, cols], in0=y_bank[:], in1=out_bias_bc[:, cols], op=ALU.add
+                    out=o_pairs[p][:, i, cols], in0=y_bank[:], in1=out_bias_bc[:, cols], op=ALU.add
                 )
 
-        def sigmoid_and_store(c):
-            for first in range(0, GROUP, 2):
-                part = o_tiles[c][:, first : first + 2, :]
-                nc.scalar.activation(out=part, in_=part, func=ACT.Sigmoid)
-                nc.sync.dma_start(out=out_rows[c][:, first : first + 2, :], in_=part)
+        def sigmoid_and_store(p):
+            nc.scalar.activation(out=o_pairs[p][:], in_=o_pairs[p][:], func=ACT.Sigmoid)
+            nc.sync.dma_start(out=out_rows[p], in_=o_pairs[p][:])
 
-        turn_x(0)
-        regroup_x(0)
-        quantise_x(0)
+        for p in pairs_of(0):
+            turn_x(p)
+            regroup_x(p)
+            quantise_x(p)
         for j in range(AHEAD):
             first_product(j)
-        turn_x(1)
-        regroup_x(1)
+        for p in pairs_of(1):
+            turn_x(p)
+            regroup_x(p)
+        bank_statistics(0)
+        mean_and_rstd(0)
 
         for c in range(-1, GROUPS + 1):
-            front, chain, back = c + 1, c, c - 1
-            if valid(chain):
-                sigmoid_of_minus_v(chain)
-            if valid(c + 2):
-                quantise_x(c + 2)
+            front, back = tiles_of(c + 1), tiles_of(c - 1)
+            for p in pairs_of(c):
+                sigmoid_of_minus_v(p)
+            for j in back:
+                multiply(j)
+            for p in pairs_of(c + 2):
+                quantise_x(p)
             for first in range(0, GROUP, 2):
-                pair = range(first, first + 2)
-                if valid(back):
-                    for a in pair:
-                        turn_h(back * GROUP + a)
-                if valid(front):
-                    for a in pair:
-                        j = front * GROUP + a
-                        statistics(j)
-                        centre_and_gain(j)
-                        if j + AHEAD < TILES:
-                            first_product(j + AHEAD)
-                if valid(back):
-                    for a in pair:
-                        regroup_h(back * GROUP + a)
-            if valid(back):
-                for a in range(GROUP):
-                    quantise_h(back * GROUP + a)
-            if valid(chain):
-                logarithm(chain)
-            if valid(c + 3):
-                turn_x(c + 3)
+                for j in back[first : first + 2]:
+                    turn_h(j)
+                for j in front[first : first + 2]:
+                    bank_statistics(j + 1)
+                    centre_and_gain(j)
+                    first_product(j + AHEAD)
+                    mean_and_rstd(j + 1)
+            for j in back:
+                quantise_h(j)
+            for p in pairs_of(c):
+                logarithm(p)
+            call_sigmoid_table()
+            for p in pairs_of(c + 3):
+                turn_x(p)
             for a in range(GROUP):
-                if valid(back):
-                    second_product(back * GROUP + a)
-                if valid(front):
-                    scale_and_bias(front * GROUP + a)
-                if valid(back):
-                    add_out_bias(back * GROUP + a)
-            if valid(chain):
-                for a in range(GROUP):
-                    tanh_and_multiply(chain, a)
-            if valid(c + 3):
-                regroup_x(c + 3)
-            if valid(back):
-                sigmoid_and_store(back)
+                for j in back[a : a + 1]:
+                    second_product(j)
+                for j in front[a : a + 1]:
+                    scale_and_bias(j)
+                for j in back[a : a + 1]:
+                    add_out_bias(j)
+            for p in pairs_of(c):
+                tanh_of_minus_log(p)
+            for p in pairs_of(c + 3):
+                regroup_x(p)
+            for p in pairs_of(c - 1):
+                sigmoid_and_store(p)

@@ -56,8 +56,8 @@ def tile_autoencoder_pb_t_kernel(
         stat_pool = stack.enter_context(tc.tile_pool(name="stat", bufs=2 * GROUP))
         centred_pool = stack.enter_context(tc.tile_pool(name="centred", bufs=GROUP))
         chain_pool = stack.enter_context(tc.tile_pool(name="chain", bufs=GROUP))
-        h_pool = stack.enter_context(tc.tile_pool(name="h", bufs=GROUP))
-        h_mx_pool = stack.enter_context(tc.tile_pool(name="h_mx", bufs=GROUP))
+        h_pool = stack.enter_context(tc.tile_pool(name="h", bufs=GROUP // 2))
+        h_mx_pool = stack.enter_context(tc.tile_pool(name="h_mx", bufs=GROUP // 2))
         out_pool = stack.enter_context(tc.tile_pool(name="o", bufs=GROUP))
         u_psum = stack.enter_context(tc.psum_pool(name="u_psum", bufs=HALVES * AHEAD))
         turn_psum = stack.enter_context(tc.psum_pool(name="turn_psum", bufs=2))
@@ -144,6 +144,8 @@ def tile_autoencoder_pb_t_kernel(
             x_groupeds[p] = grouped
 
         def quantise_x(p):
+            if p >= PAIRS:
+                return
             codes = x_mx_pool.tile([P, 2 * P], U32, align_bytes=64)
             scales = x_mx_pool.tile([P, 2 * P], U8, align_bytes=64)
             nc.vector.quantize_mx(
@@ -224,7 +226,7 @@ def tile_autoencoder_pb_t_kernel(
             )
 
         t_pairs = {}
-        h_tiles = {}
+        h_pairs = {}
 
         def sigmoid_of_minus_v(p):
             t_pair = chain_pool.tile([P, 2, N1], F32)
@@ -242,20 +244,18 @@ def tile_autoencoder_pb_t_kernel(
         def tanh_of_minus_log(p):
             nc.scalar.activation(out=t_pairs[p][:], in_=t_pairs[p][:], func=ACT.Tanh, scale=-1.0)
 
-        def multiply(j):
-            p, i = divmod(j, 2)
-            h_bf = h_pool.tile([P, N1], BF16)
-            nc.vector.tensor_tensor(
-                out=h_bf[:], in0=v_pairs[p][:, i, :], in1=t_pairs[p][:, i, :], op=ALU.mult
-            )
-            h_tiles[j] = h_bf
+        def multiply(p):
+            h_pair = h_pool.tile([P, 2, N1], BF16)
+            nc.vector.tensor_tensor(out=h_pair[:], in0=v_pairs[p][:], in1=t_pairs[p][:], op=ALU.mult)
+            h_pairs[p] = h_pair
 
         h_groupeds = {}
         h_codes = {}
         h_scales = {}
 
-        def turn_h(j):
-            words = h_tiles[j][:].bitcast(F32)
+        def turn_h(j, copy_out):
+            p, i = divmod(j, 2)
+            words = h_pairs[p][:, i, :].bitcast(F32)
             h_bank = turn_psum.tile([P, PASSES2, 2, P], F32, tag="turn")
             for g in range(PASSES2):
                 for e2 in range(2):
@@ -264,21 +264,26 @@ def tile_autoencoder_pb_t_kernel(
                         words[:, g * K_PASS // 2 + e2 : (g + 1) * K_PASS // 2 : 2],
                         identity[:],
                     )
-            grouped = h_mx_pool.tile([P, PASSES2 * P * PACK], BF16, align_bytes=64)
-            nc.scalar.copy(
-                out=grouped[:].bitcast(F32).rearrange("q (g r e2) -> q g r e2", g=PASSES2, e2=2),
+            if i == 0:
+                grouped = h_mx_pool.tile([P, 2, PASSES2 * P * PACK], BF16, align_bytes=64)
+                h_groupeds[p] = grouped
+            copy_out(
+                out=h_groupeds[p][:, i, :]
+                .bitcast(F32)
+                .rearrange("q (g r e2) -> q g r e2", g=PASSES2, e2=2),
                 in_=h_bank[:].rearrange("q g e2 r -> q g r e2"),
             )
-            h_groupeds[j] = grouped
 
-        def quantise_h(j):
-            codes = h_mx_pool.tile([P, PASSES2 * P], U32, align_bytes=64)
-            scales = h_mx_pool.tile([P, PASSES2 * P], U8, align_bytes=64)
+        def quantise_h(p):
+            codes = h_mx_pool.tile([P, 2 * PASSES2 * P], U32, align_bytes=64)
+            scales = h_mx_pool.tile([P, 2 * PASSES2 * P], U8, align_bytes=64)
             nc.vector.quantize_mx(
-                out=codes[:].bitcast(FP8X4), scales=scales[:], in_=h_groupeds[j][:]
+                out=codes[:].bitcast(FP8X4),
+                scales=scales[:],
+                in_=h_groupeds[p][:].rearrange("q i w -> q (i w)"),
             )
-            h_codes[j] = codes
-            h_scales[j] = scales
+            h_codes[p] = codes
+            h_scales[p] = scales
 
         y_banks = {}
         o_pairs = {}
@@ -288,13 +293,14 @@ def tile_autoencoder_pb_t_kernel(
             y_wide = y_psum.tile([P, BANK], F32)
             y_narrow = y_psum.tile([P, N2 - BANK], F32)
             y_banks[j] = (y_wide, y_narrow)
+            p, i = divmod(j, 2)
             for g in range(PASSES2):
-                rows = slice(g * P, (g + 1) * P)
+                rows = slice((i * PASSES2 + g) * P, (i * PASSES2 + g + 1) * P)
                 for y_bank, cols in zip(y_banks[j], y_columns):
                     nc.tensor.matmul_mx(
                         out=y_bank[:],
-                        lhsT=h_codes[j][:, rows].bitcast(FP8X4),
-                        lhsT_scale=h_scales[j][:, rows],
+                        lhsT=h_codes[p][:, rows].bitcast(FP8X4),
+                        lhsT_scale=h_scales[p][:, rows],
                         rhs=w3_words[:, g, cols].bitcast(FP8X4),
                         rhs_scale=w3_scales[:, g, cols],
                         start=(g == 0),
@@ -315,36 +321,36 @@ def tile_autoencoder_pb_t_kernel(
             nc.scalar.activation(out=o_pairs[p][:], in_=o_pairs[p][:], func=ACT.Sigmoid)
             nc.sync.dma_start(out=out_rows[p], in_=o_pairs[p][:])
 
-        for p in pairs_of(0):
-            turn_x(p)
-            regroup_x(p)
-            quantise_x(p)
+        turn_x(0)
+        regroup_x(0)
+        quantise_x(0)
         for j in range(AHEAD):
             first_product(j)
-        for p in pairs_of(1):
-            turn_x(p)
-            regroup_x(p)
         bank_statistics(0)
         mean_and_rstd(0)
+        for p in (pairs_of(0) + pairs_of(1))[1:]:
+            turn_x(p)
+            regroup_x(p)
 
         for c in range(-1, GROUPS + 1):
             front, back = tiles_of(c + 1), tiles_of(c - 1)
+            copy_out = nc.scalar.copy if front else nc.vector.tensor_copy
             for p in pairs_of(c):
                 sigmoid_of_minus_v(p)
-            for j in back:
-                multiply(j)
-            for p in pairs_of(c + 2):
-                quantise_x(p)
+            for p in pairs_of(c - 1):
+                multiply(p)
             for first in range(0, GROUP, 2):
                 for j in back[first : first + 2]:
-                    turn_h(j)
+                    turn_h(j, copy_out)
+                for j in front[first : first + 1]:
+                    quantise_x(j // 2 + 1)
                 for j in front[first : first + 2]:
                     bank_statistics(j + 1)
                     centre_and_gain(j)
                     first_product(j + AHEAD)
                     mean_and_rstd(j + 1)
-            for j in back:
-                quantise_h(j)
+            for p in pairs_of(c - 1):
+                quantise_h(p)
             for p in pairs_of(c):
                 logarithm(p)
             call_sigmoid_table()

@@ -29,6 +29,8 @@ PAIRS = TILES // 2
 GROUP = 4
 GROUPS = TILES // GROUP
 AHEAD = 2
+TURN_STEPS = GROUP // 2
+STEPS = GROUP + 2
 LOG_FLOOR = 2.0**-60
 
 FLOPS = 2 * ROWS * K1 * N1 + 2 * ROWS * N1 * N2
@@ -40,6 +42,10 @@ def tiles_of(c):
 
 def pairs_of(c):
     return [j // 2 for j in tiles_of(c)[::2]]
+
+
+def item(sequence, i):
+    return sequence[i : i + 1] if i >= 0 else []
 
 
 def tile_autoencoder_pb_t_kernel(
@@ -332,37 +338,41 @@ def tile_autoencoder_pb_t_kernel(
             turn_x(p)
             regroup_x(p)
 
-        for c in range(-1, GROUPS + 1):
+        def step(c, a, copy_out):
             front, back = tiles_of(c + 1), tiles_of(c - 1)
-            copy_out = nc.scalar.copy if front else nc.vector.tensor_copy
+            for j in back[2 * a : 2 * a + 2]:
+                turn_h(j, copy_out)
+            for j in item(front, a):
+                if j % 2 == 0:
+                    quantise_x(j // 2 + 1)
+                bank_statistics(j + 1)
+                centre_and_gain(j)
+                first_product(j + AHEAD)
+                mean_and_rstd(j + 1)
+            for p in item(pairs_of(c - 1), a - 1):
+                quantise_h(p)
+            for j in item(back, a - 2):
+                add_out_bias(j)
+            for j in item(back, a - 1):
+                second_product(j)
+            for j in item(front, a - 2):
+                scale_and_bias(j)
+
+        for c in range(-1, GROUPS + 1):
+            copy_out = nc.scalar.copy if tiles_of(c + 1) else nc.vector.tensor_copy
             for p in pairs_of(c):
                 sigmoid_of_minus_v(p)
             for p in pairs_of(c - 1):
                 multiply(p)
-            for first in range(0, GROUP, 2):
-                for j in back[first : first + 2]:
-                    turn_h(j, copy_out)
-                for j in front[first : first + 1]:
-                    quantise_x(j // 2 + 1)
-                for j in front[first : first + 2]:
-                    bank_statistics(j + 1)
-                    centre_and_gain(j)
-                    first_product(j + AHEAD)
-                    mean_and_rstd(j + 1)
-            for p in pairs_of(c - 1):
-                quantise_h(p)
+            for a in range(TURN_STEPS):
+                step(c, a, copy_out)
+            for p in pairs_of(c + 3):
+                turn_x(p)
             for p in pairs_of(c):
                 logarithm(p)
             call_sigmoid_table()
-            for p in pairs_of(c + 3):
-                turn_x(p)
-            for a in range(GROUP):
-                for j in back[a : a + 1]:
-                    second_product(j)
-                for j in front[a : a + 1]:
-                    scale_and_bias(j)
-                for j in back[a : a + 1]:
-                    add_out_bias(j)
+            for a in range(TURN_STEPS, STEPS):
+                step(c, a, copy_out)
             for p in pairs_of(c):
                 tanh_of_minus_log(p)
             for p in pairs_of(c + 3):

from contextlib import ExitStack

import concourse.mybir as mybir
from concourse.masks import make_identity

F32 = mybir.dt.float32
BF16 = mybir.dt.bfloat16
U8 = mybir.dt.uint8
U32 = mybir.dt.uint32
I32 = mybir.dt.int32
FP8X4 = mybir.dt.float8_e4m3fn_x4
ACT = mybir.ActivationFunctionType
ALU = mybir.AluOpType

P = 128
PACK = 4
K_PASS = P * PACK
BANK = 512

ROWS = 4096
K1 = 512
N1 = 1024
N2 = 768
PASSES2 = N1 // K_PASS
HALVES = N1 // BANK
EPS = 1e-5
TILES = ROWS // P
PAIRS = TILES // 2
GROUP = 4
GROUPS = TILES // GROUP
AHEAD = 2
TURN_STEPS = GROUP // 2
STEPS = GROUP + 2
LOG_FLOOR = 2.0**-60

FLOPS = 2 * ROWS * K1 * N1 + 2 * ROWS * N1 * N2


def tiles_of(c):
    return [c * GROUP + a for a in range(GROUP)] if 0 <= c < GROUPS else []


def pairs_of(c):
    return [j // 2 for j in tiles_of(c)[::2]]


def item(sequence, i):
    return sequence[i : i + 1] if i >= 0 else []


def tile_autoencoder_pb_t_kernel(
    tc, h_dec1, D2_words, D2_scales, g4, b4, D3_words, D3_scales, bo, out
):
    nc = tc.nc
    x_rows = h_dec1.rearrange("(p r i) k -> p r i k", r=P, i=2)
    out_rows = out.rearrange("(p r i) n -> p r i n", r=P, i=2)

    with ExitStack() as stack:
        const = stack.enter_context(tc.tile_pool(name="const", bufs=1))
        x_pool = stack.enter_context(tc.tile_pool(name="x", bufs=PAIRS))
        x_mx_pool = stack.enter_context(tc.tile_pool(name="x_mx", bufs=3 * GROUP // 2))
        stat_pool = stack.enter_context(tc.tile_pool(name="stat", bufs=2 * GROUP))
        centred_pool = stack.enter_context(tc.tile_pool(name="centred", bufs=GROUP))
        chain_pool = stack.enter_context(tc.tile_pool(name="chain", bufs=GROUP))
        h_pool = stack.enter_context(tc.tile_pool(name="h", bufs=GROUP // 2))
        h_mx_pool = stack.enter_context(tc.tile_pool(name="h_mx", bufs=GROUP // 2))
        out_pool = stack.enter_context(tc.tile_pool(name="o", bufs=GROUP))
        u_psum = stack.enter_context(tc.psum_pool(name="u_psum", bufs=HALVES * AHEAD))
        turn_psum = stack.enter_context(tc.psum_pool(name="turn_psum", bufs=2))
        y_psum = stack.enter_context(tc.psum_pool(name="y_psum", bufs=1))
        stack.enter_context(tc.manual_schedule())

        identity = const.tile([P, P], F32)
        make_identity(nc, identity[:])
        log_floor = const.tile([P, 1], F32)
        nc.vector.memset(log_floor[:], LOG_FLOOR)
        minus_half = const.tile([P, 1], F32)
        nc.vector.memset(minus_half[:], -0.5)
        table_scratch = const.tile([P, 1], F32)

        w2_words = const.tile([P, N1], U32, align_bytes=64)
        w2_scales = const.tile([P, N1], U8, align_bytes=64)
        w3_words = const.tile([P, PASSES2, N2], U32, align_bytes=64)
        w3_scales = const.tile([P, PASSES2, N2], U8, align_bytes=64)
        nc.vector.memset(w2_scales[:].bitcast(I32), 0)
        nc.vector.memset(w3_scales[:].bitcast(I32), 0)

        x_tiles = {}

        def load_x(p):
            x_sb = x_pool.tile([P, 2, K1], BF16)
            nc.sync.dma_start(out=x_sb[:], in_=x_rows[p])
            x_tiles[p] = x_sb

        def load_scales(plane, rows):
            for quadrant in range(4):
                nc.sync.dma_start(
                    out=plane[32 * quadrant : 32 * quadrant + 4, :].bitcast(I32),
                    in_=rows[4 * quadrant : 4 * quadrant + 4, :].bitcast(I32),
                )

        def load_words(words, packed):
            nc.sync.dma_start(
                out=words.bitcast(I32),
                in_=packed.rearrange("p n t -> p (n t)").bitcast(I32),
            )

        for p in pairs_of(0):
            load_x(p)
        load_scales(w2_scales, D2_scales[0])
        load_words(w2_words[:], D2_words[0])
        for p in pairs_of(1) + pairs_of(2):
            load_x(p)
        for g in range(PASSES2):
            load_scales(w3_scales[:, g, :], D3_scales[g])
        for g in range(PASSES2):
            load_words(w3_words[:, g, :], D3_words[g])
        for c in range(3, GROUPS):
            for p in pairs_of(c):
                load_x(p)

        gain_bc = const.tile([P, N1], BF16)
        nc.scalar.dma_start(out=gain_bc[:], in_=g4.partition_broadcast(P))
        bias_bc = const.tile([P, N1], BF16)
        nc.scalar.dma_start(out=bias_bc[:], in_=b4.partition_broadcast(P))
        out_bias_bc = const.tile([P, N2], BF16)
        nc.scalar.dma_start(out=out_bias_bc[:], in_=bo.partition_broadcast(P))

        x_turned = {}
        x_groupeds = {}
        x_codes = {}
        x_scales = {}

        def turn_x(p):
            words = x_tiles[p][:].bitcast(F32)
            x_bank = turn_psum.tile([P, 2, 2 * P], F32, tag="turn")
            for i in range(2):
                for e2 in range(2):
                    nc.tensor.transpose(
                        x_bank[:, e2, i * P : (i + 1) * P], words[:, i, e2 : K1 // 2 : 2], identity[:]
                    )
            x_turned[p] = x_bank

        def regroup_x(p):
            grouped = x_mx_pool.tile([P, 2 * P * PACK], BF16, align_bytes=64)
            nc.scalar.copy(
                out=grouped[:].bitcast(F32).rearrange("q (w e2) -> q w e2", e2=2),
                in_=x_turned[p][:].rearrange("q e2 w -> q w e2"),
            )
            x_groupeds[p] = grouped

        def quantise_x(p):
            if p >= PAIRS:
                return
            codes = x_mx_pool.tile([P, 2 * P], U32, align_bytes=64)
            scales = x_mx_pool.tile([P, 2 * P], U8, align_bytes=64)
            nc.vector.quantize_mx(
                out=codes[:].bitcast(FP8X4), scales=scales[:], in_=x_groupeds[p][:]
            )
            x_codes[p] = codes
            x_scales[p] = scales

        u_banks = {}
        stats_of = {}
        mean_vars = {}
        rstds = {}
        centreds = {}
        v_pairs = {}

        def first_product(j):
            if j >= TILES:
                return
            p, i = divmod(j, 2)
            rows = slice(i * P, (i + 1) * P)
            banks = []
            for half in range(HALVES):
                cols = slice(half * BANK, (half + 1) * BANK)
                u_bank = u_psum.tile([P, BANK], F32, tag="u")
                nc.tensor.matmul_mx(
                    out=u_bank[:],
                    lhsT=x_codes[p][:, rows].bitcast(FP8X4),
                    lhsT_scale=x_scales[p][:, rows],
                    rhs=w2_words[:, cols].bitcast(FP8X4),
                    rhs_scale=w2_scales[:, cols],
                    start=True,
                    stop=True,
                )
                banks.append(u_bank)
            u_banks[j] = banks

        def bank_statistics(j):
            if j >= TILES:
                return
            stats = stat_pool.tile([P, HALVES, 6], F32)
            for half in range(HALVES):
                nc.vector.bn_stats(out=stats[:, half, :], in_=u_banks[j][half][:])
            stats_of[j] = stats

        def mean_and_rstd(j):
            if j >= TILES:
                return
            mean_var = stat_pool.tile([P, 2], F32)
            nc.vector.bn_aggr(out=mean_var[:], in_=stats_of[j][:].rearrange("r h s -> r (h s)"))
            var_eps = stat_pool.tile([P, 1], F32)
            nc.gpsimd.tensor_scalar(
                out=var_eps[:], in0=mean_var[:, 1:2], scalar1=1.0, scalar2=EPS,
                op0=ALU.mult, op1=ALU.add,
            )
            rstd = stat_pool.tile([P, 1], F32)
            nc.gpsimd.tensor_tensor(out=rstd[:], in0=var_eps[:], in1=minus_half[:], op=ALU.pow)
            mean_vars[j] = mean_var
            rstds[j] = rstd

        def centre_and_gain(j):
            centred = centred_pool.tile([P, N1], F32)
            for half in range(HALVES):
                cols = slice(half * BANK, (half + 1) * BANK)
                nc.vector.scalar_tensor_tensor(
                    out=centred[:, cols], in0=u_banks[j][half][:], scalar=mean_vars[j][:, 0:1],
                    in1=gain_bc[:, cols], op0=ALU.subtract, op1=ALU.mult,
                )
            centreds[j] = centred

        def scale_and_bias(j):
            p, i = divmod(j, 2)
            if i == 0:
                v_pair = chain_pool.tile([P, 2, N1], F32)
                v_pairs[p] = v_pair
            nc.vector.scalar_tensor_tensor(
                out=v_pairs[p][:, i, :], in0=centreds[j][:], scalar=rstds[j][:, 0:1],
                in1=bias_bc[:], op0=ALU.mult, op1=ALU.add,
            )

        t_pairs = {}
        h_pairs = {}

        def sigmoid_of_minus_v(p):
            t_pair = chain_pool.tile([P, 2, N1], F32)
            nc.scalar.activation(out=t_pair[:], in_=v_pairs[p][:], func=ACT.Sigmoid, scale=-1.0)
            t_pairs[p] = t_pair

        def logarithm(p):
            nc.scalar.activation(
                out=t_pairs[p][:], in_=t_pairs[p][:], func=ACT.Ln, bias=log_floor[:, 0:1]
            )

        def call_sigmoid_table():
            nc.scalar.activation(out=table_scratch[:], in_=log_floor[:], func=ACT.Sigmoid)

        def tanh_of_minus_log(p):
            nc.scalar.activation(out=t_pairs[p][:], in_=t_pairs[p][:], func=ACT.Tanh, scale=-1.0)

        def multiply(p):
            h_pair = h_pool.tile([P, 2, N1], BF16)
            nc.vector.tensor_tensor(out=h_pair[:], in0=v_pairs[p][:], in1=t_pairs[p][:], op=ALU.mult)
            h_pairs[p] = h_pair

        h_groupeds = {}
        h_codes = {}
        h_scales = {}

        def turn_h(j, copy_out):
            p, i = divmod(j, 2)
            words = h_pairs[p][:, i, :].bitcast(F32)
            h_bank = turn_psum.tile([P, PASSES2, 2, P], F32, tag="turn")
            for g in range(PASSES2):
                for e2 in range(2):
                    nc.tensor.transpose(
                        h_bank[:, g, e2, :],
                        words[:, g * K_PASS // 2 + e2 : (g + 1) * K_PASS // 2 : 2],
                        identity[:],
                    )
            if i == 0:
                grouped = h_mx_pool.tile([P, 2, PASSES2 * P * PACK], BF16, align_bytes=64)
                h_groupeds[p] = grouped
            copy_out(
                out=h_groupeds[p][:, i, :]
                .bitcast(F32)
                .rearrange("q (g r e2) -> q g r e2", g=PASSES2, e2=2),
                in_=h_bank[:].rearrange("q g e2 r -> q g r e2"),
            )

        def quantise_h(p):
            codes = h_mx_pool.tile([P, 2 * PASSES2 * P], U32, align_bytes=64)
            scales = h_mx_pool.tile([P, 2 * PASSES2 * P], U8, align_bytes=64)
            nc.vector.quantize_mx(
                out=codes[:].bitcast(FP8X4),
                scales=scales[:],
                in_=h_groupeds[p][:].rearrange("q i w -> q (i w)"),
            )
            h_codes[p] = codes
            h_scales[p] = scales

        y_banks = {}
        o_pairs = {}
        y_columns = (slice(0, BANK), slice(BANK, N2))

        def second_product(j):
            y_wide = y_psum.tile([P, BANK], F32)
            y_narrow = y_psum.tile([P, N2 - BANK], F32)
            y_banks[j] = (y_wide, y_narrow)
            p, i = divmod(j, 2)
            for g in range(PASSES2):
                rows = slice((i * PASSES2 + g) * P, (i * PASSES2 + g + 1) * P)
                for y_bank, cols in zip(y_banks[j], y_columns):
                    nc.tensor.matmul_mx(
                        out=y_bank[:],
                        lhsT=h_codes[p][:, rows].bitcast(FP8X4),
                        lhsT_scale=h_scales[p][:, rows],
                        rhs=w3_words[:, g, cols].bitcast(FP8X4),
                        rhs_scale=w3_scales[:, g, cols],
                        start=(g == 0),
                        stop=(g == PASSES2 - 1),
                    )

        def add_out_bias(j):
            p, i = divmod(j, 2)
            if i == 0:
                o_pair = out_pool.tile([P, 2, N2], F32)
                o_pairs[p] = o_pair
            for y_bank, cols in zip(y_banks[j], y_columns):
                nc.vector.tensor_tensor(
                    out=o_pairs[p][:, i, cols], in0=y_bank[:], in1=out_bias_bc[:, cols], op=ALU.add
                )

        def sigmoid_and_store(p):
            nc.scalar.activation(out=o_pairs[p][:], in_=o_pairs[p][:], func=ACT.Sigmoid)
            nc.sync.dma_start(out=out_rows[p], in_=o_pairs[p][:])

        turn_x(0)
        regroup_x(0)
        quantise_x(0)
        for j in range(AHEAD):
            first_product(j)
        bank_statistics(0)
        mean_and_rstd(0)
        for p in (pairs_of(0) + pairs_of(1))[1:]:
            turn_x(p)
            regroup_x(p)

        def step(c, a, copy_out):
            front, back = tiles_of(c + 1), tiles_of(c - 1)
            for j in back[2 * a : 2 * a + 2]:
                turn_h(j, copy_out)
            for j in item(front, a):
                if j % 2 == 0:
                    quantise_x(j // 2 + 1)
                bank_statistics(j + 1)
                centre_and_gain(j)
                first_product(j + AHEAD)
                mean_and_rstd(j + 1)
            for p in item(pairs_of(c - 1), a - 1):
                quantise_h(p)
            for j in item(back, a - 2):
                add_out_bias(j)
            for j in item(back, a - 1):
                second_product(j)
            for j in item(front, a - 2):
                scale_and_bias(j)

        for c in range(-1, GROUPS + 1):
            copy_out = nc.scalar.copy if tiles_of(c + 1) else nc.vector.tensor_copy
            for p in pairs_of(c):
                sigmoid_of_minus_v(p)
            for p in pairs_of(c - 1):
                multiply(p)
            for a in range(TURN_STEPS):
                step(c, a, copy_out)
            for p in pairs_of(c + 3):
                turn_x(p)
            for p in pairs_of(c):
                logarithm(p)
            call_sigmoid_table()
            for a in range(TURN_STEPS, STEPS):
                step(c, a, copy_out)
            for p in pairs_of(c):
                tanh_of_minus_log(p)
            for p in pairs_of(c + 3):
                regroup_x(p)
            for p in pairs_of(c - 1):
                sigmoid_and_store(p)
